import numpy as np
import ml_dtypes


def mxq(x, axis, fmt="e4m3"):
    dtype, down = {"e4m3": (ml_dtypes.float8_e4m3fn, 7), "e5m2": (ml_dtypes.float8_e5m2, 14)}[fmt]
    v = np.moveaxis(np.asarray(x, np.float32).astype(ml_dtypes.bfloat16).astype(np.float64), axis, -1)
    blocks = v.reshape(v.shape[:-1] + (-1, 32))
    amax = np.abs(blocks).max(-1, keepdims=True)
    byte = np.maximum(np.where(amax > 0, np.frexp(amax)[1] - 1 + 127, 0) - down, 1)
    scale = np.exp2(byte - 127.0)
    codes = (blocks / scale).astype(np.float32).astype(dtype).astype(np.float64)
    return np.moveaxis((codes * scale).reshape(v.shape), -1, axis)


WIDE = False


def mx_kscale(k):
    if not WIDE:
        return np.ones(k)
    levels = np.array([20, -20, 10, -10, 0])
    a = np.random.permutation(np.resize(levels, k // 512 * 4)).reshape(k // 512, 4)
    idx = np.arange(k)
    return np.exp2(a[idx // 512, idx % 128 // 32])


BF16 = ml_dtypes.bfloat16


def bf(x):
    return np.asarray(x, np.float32).astype(BF16)


def f64(x):
    return np.asarray(x).astype(np.float64)


B, S, D_IN, D_OUT = 2, 1024, 1024, 1024


def quant8(w):
    mv = np.max(np.abs(w))
    q = np.ceil(np.log2(mv)) - 6.0
    scale = np.exp2(q)
    return np.round(w / scale) * scale


def setup_inputs():
    u = mx_kscale(D_OUT)
    x = np.random.standard_normal((B, S, D_IN))
    weight = np.random.standard_normal((D_OUT, D_IN)) * 3.0 / np.sqrt(D_IN)
    w_upper = quant8(weight)
    w_lower = weight - w_upper
    g = np.random.standard_normal((B, S, D_OUT)) * np.exp2(np.random.randint(-12, 1, (B, S, 1))) * u
    return {"x": bf(x), "weight_upper": bf(w_upper / u[:, None]), "weight_lower": bf(w_lower / u[:, None]), "grad_out": bf(g)}


def reference(x, weight_upper, weight_lower, grad_out):
    gq = mxq(f64(grad_out), 2, "e5m2")
    g_upper = gq @ mxq(f64(weight_upper), 0, "e4m3")
    g_lower = gq @ mxq(f64(weight_lower), 0, "e4m3")
    return g_upper + g_lower

@@ -1,0 +1,185 @@
+from contextlib import ExitStack
+
+import concourse.masks as masks
+import concourse.mybir as mybir
+
+FLOPS = 2 * 2 * 2048 * 1024 * 1024
+BYTES = 2048 * 1024 * 2 + 2 * 1024 * 1024 * 2 + 2048 * 1024 * 4
+
+F32 = mybir.dt.float32
+BF16 = mybir.dt.bfloat16
+U32 = mybir.dt.uint32
+U8 = mybir.dt.uint8
+E4X4 = mybir.dt.float8_e4m3fn_x4
+E5X4 = mybir.dt.float8_e5m2_x4
+
+P = 128
+HALF = 512
+V_COLS = 336
+
+
+def tile_virtual16bmatmul_t_kernel(tc, x, weight_upper, weight_lower, grad_out, out):
+    nc = tc.nc
+    g_rows = grad_out.flatten_outer_dims()
+    o_rows = out.flatten_outer_dims()
+    g_late = g_rows[1024:2048, :].rearrange("(p j) k -> p j k", j=8)
+    o_late = o_rows[1024:2048, :].rearrange("(p j) n -> p j n", j=8)
+    weights = (weight_upper, weight_lower)
+
+    with ExitStack() as ctx:
+        ctx.enter_context(tc.manual_schedule())
+        keep = ctx.enter_context(tc.tile_pool(name="keep", bufs=1))
+        wgrp_pool = ctx.enter_context(tc.tile_pool(name="wgrp", bufs=3))
+        ggrp_pool = ctx.enter_context(tc.tile_pool(name="ggrp", bufs=4))
+        psum = ctx.enter_context(tc.psum_pool(name="psum", bufs=1))
+
+        ident = keep.tile([P, P], F32, name="ident")
+        masks.make_identity(nc, ident[:])
+
+        wraw = {}
+        wgrp = {}
+        wcodes = {}
+        wscales = {}
+        gwords = {}
+        ggrp = {}
+        gcodes = {}
+        gscales = {}
+        banks = {}
+
+        def load_w(c):
+            h, g, w = c // 4, (c // 2) % 2, c % 2
+            raw = keep.tile([P, 4, HALF], BF16, name="wraw%d" % c)
+            for u in range(2):
+                r0 = 512 * g + 256 * u
+                nc.sync.dma_start(
+                    out=raw[:, 2 * u : 2 * u + 2, :],
+                    in_=weights[w][r0 : r0 + 256, HALF * h : HALF * (h + 1)].rearrange("(p e) c -> p e c", e=2),
+                )
+            wraw[c] = raw
+
+        def load_g_early(t):
+            raw = keep.tile([P, 1024], BF16, name="graw%d" % t)
+            nc.sync.dma_start(out=raw[:], in_=g_rows[P * t : P * (t + 1), :])
+            gwords[t] = raw[:].bitcast(F32)
+
+        def load_g_late(i):
+            raw = keep.tile([P, 4096], BF16, name="glate%d" % i)
+            nc.sync.dma_start(out=raw[:], in_=g_late[:, 4 * i : 4 * i + 4, :].rearrange("p j k -> p (j k)"))
+            for jj in range(4):
+                gwords[8 + 4 * i + jj] = raw[:].bitcast(F32)[:, 512 * jj : 512 * (jj + 1)]
+
+        def regroup_w(c, copy, lo, hi):
+            if c not in wgrp:
+                wgrp[c] = wgrp_pool.tile([P, HALF, 4], BF16, name="wgrp%d" % c, tag="wgrp", align_bytes=64)
+            copy(
+                out=wgrp[c][:, lo:hi, :].rearrange("p (c i) t -> p c t i", i=4),
+                in_=wraw[c][:, :, lo:hi].rearrange("p t (c i) -> p c t i", i=4),
+            )
+
+        def regroup_w_vector(c):
+            regroup_w(c, nc.vector.tensor_copy, 0, V_COLS)
+
+        def regroup_w_scalar(c):
+            regroup_w(c, nc.scalar.copy, V_COLS, HALF)
+
+        def quantise_w(c):
+            wcodes[c] = keep.tile([P, HALF], U32, name="wcodes%d" % c, align_bytes=64)
+            wscales[c] = keep.tile([P, HALF], U8, name="wscales%d" % c, align_bytes=64)
+            nc.vector.quantize_mx(
+                out=wcodes[c][:].bitcast(E4X4),
+                scales=wscales[c][:],
+                in_=wgrp[c][:].rearrange("p c t -> p (c t)"),
+            )
+
+        def prepare_w(c):
+            regroup_w_vector(c)
+            regroup_w_scalar(c)
+            quantise_w(c)
+
+        def prepare_g(t):
+            xt = psum.tile([P, 4, P], F32, name="xt%d" % t, tag="bank%d" % (t % 8))
+            for j in range(4):
+                nc.tensor.transpose(xt[:, j, :], gwords[t][:, P * j : P * (j + 1)], ident[:])
+            grp = ggrp_pool.tile([P, 1024], BF16, name="ggrp%d" % t, tag="ggrp", align_bytes=64)
+            nc.scalar.copy(
+                out=grp[:].bitcast(F32).rearrange("p (g r u) -> p g r u", g=2, u=2),
+                in_=xt[:].rearrange("p (g u) r -> p g r u", u=2),
+            )
+            gcodes[t] = keep.tile([P, 256], U32, name="gcodes%d" % t, align_bytes=64)
+            gscales[t] = keep.tile([P, 256], U8, name="gscales%d" % t, align_bytes=64)
+            nc.vector.quantize_mx(out=gcodes[t][:].bitcast(E5X4), scales=gscales[t][:], in_=grp[:])
+
+        def mx_pass(acc, t, c):
+            g = (c // 2) % 2
+            nc.tensor.matmul_mx(
+                out=acc[:],
+                lhsT=gcodes[t][:, P * g : P * (g + 1)].bitcast(E5X4),
+                lhsT_scale=gscales[t][:, P * g : P * (g + 1)],
+                rhs=wcodes[c][:].bitcast(E4X4),
+                rhs_scale=wscales[c][:],
+                start=(c % 4 == 0),
+                stop=(c % 4 == 3),
+            )
+
+        def empty_early(t, h, copy):
+            stage = keep.tile([P, HALF], F32, name="o%d_%d" % (t, h))
+            copy(out=stage[:], in_=banks[t][:])
+            nc.sync.dma_start(out=o_rows[P * t : P * (t + 1), HALF * h : HALF * (h + 1)], in_=stage[:])
+
+        load_w(0)
+        for t in range(8):
+            load_g_early(t)
+        for c in range(1, 8):
+            load_w(c)
+        for i in range(2):
+            load_g_late(i)
+
+        prepare_w(0)
+        for t in range(8):
+            prepare_g(t)
+
+        for c in range(4):
+            prepare_w(c + 1)
+            for t in range(8):
+                if c == 0:
+                    banks[t] = psum.tile([P, HALF], F32, name="accA%d" % t, tag="bank%d" % t)
+                mx_pass(banks[t], t, c)
+        prepare_w(5)
+        empty_early(0, 0, nc.scalar.copy)
+        empty_early(1, 0, nc.scalar.copy)
+        empty_early(2, 0, nc.vector.tensor_copy)
+        regroup_w_vector(6)
+        empty_early(3, 0, nc.scalar.copy)
+        empty_early(4, 0, nc.scalar.copy)
+        empty_early(5, 0, nc.vector.tensor_copy)
+        empty_early(6, 0, nc.scalar.copy)
+        empty_early(7, 0, nc.vector.tensor_copy)
+        regroup_w_scalar(6)
+        quantise_w(6)
+        prepare_w(7)
+
+        for c in range(4, 8):
+            for t in range(8):
+                if c == 4:
+                    banks[t] = psum.tile([P, HALF], F32, name="accB%d" % t, tag="bank%d" % t)
+                mx_pass(banks[t], t, c)
+        for t in range(8):
+            empty_early(t, 1, nc.scalar.copy if t % 2 == 0 else nc.vector.tensor_copy)
+
+        for t in range(8, 16):
+            prepare_g(t)
+        for t in range(8, 16):
+            stage = keep.tile([P, 2 * HALF], F32, name="o%d" % t)
+            for h in range(2):
+                q = 2 * (t - 8) + h
+                acc = psum.tile([P, HALF], F32, name="accC%d" % q, tag="bank%d" % (q % 8))
+                for c in range(4 * h, 4 * h + 4):
+                    mx_pass(acc, t, c)
+                copy = nc.scalar.copy if h == 0 else nc.vector.tensor_copy
+                copy(out=stage[:, HALF * h : HALF * (h + 1)], in_=acc[:])
+                if t == 15:
+                    nc.sync.dma_start(
+                        out=o_late[:, t - 8, HALF * h : HALF * (h + 1)], in_=stage[:, HALF * h : HALF * (h + 1)]
+                    )
+            if t < 15:
+                nc.sync.dma_start(out=o_late[:, t - 8, :], in_=stage[:])

@@ -147,22 +147,23 @@ def tile_virtual16bmatmul_t_kernel(tc, x, weight_upper, weight_lower, grad_out, 
         prepare_w(5)
         empty_early(0, 0, nc.scalar.copy)
         empty_early(1, 0, nc.scalar.copy)
-        empty_early(2, 0, nc.vector.tensor_copy)
-        regroup_w_vector(6)
+        prepare_w(6)
+        empty_early(2, 0, nc.scalar.copy)
         empty_early(3, 0, nc.scalar.copy)
-        empty_early(4, 0, nc.scalar.copy)
-        empty_early(5, 0, nc.vector.tensor_copy)
-        empty_early(6, 0, nc.scalar.copy)
-        empty_early(7, 0, nc.vector.tensor_copy)
-        regroup_w_scalar(6)
-        quantise_w(6)
-        prepare_w(7)
+        empty_early(4, 0, nc.vector.tensor_copy)
+        regroup_w_vector(7)
+        regroup_w_scalar(7)
+        empty_early(5, 0, nc.scalar.copy)
+        empty_early(6, 0, nc.vector.tensor_copy)
+        empty_early(7, 0, nc.scalar.copy)
+        quantise_w(7)
 
-        for c in range(4, 8):
+        for first in (4, 6):
             for t in range(8):
-                if c == 4:
+                if first == 4:
                     banks[t] = psum.tile([P, HALF], F32, name="accB%d" % t, tag="bank%d" % t)
-                mx_pass(banks[t], t, c)
+                mx_pass(banks[t], t, first)
+                mx_pass(banks[t], t, first + 1)
         for t in range(8):
             empty_early(t, 1, nc.scalar.copy if t % 2 == 0 else nc.vector.tensor_copy)
 

@@ -15,6 +15,7 @@ E5X4 = mybir.dt.float8_e5m2_x4
 
 P = 128
 HALF = 512
+PAD = 48
 V_COLS = 336
 
 
@@ -83,8 +84,8 @@ def tile_virtual16bmatmul_t_kernel(tc, x, weight_upper, weight_lower, grad_out, 
             regroup_w(c, nc.scalar.copy, V_COLS, HALF)
 
         def quantise_w(c):
-            wcodes[c] = keep.tile([P, HALF], U32, name="wcodes%d" % c, align_bytes=64)
-            wscales[c] = keep.tile([P, HALF], U8, name="wscales%d" % c, align_bytes=64)
+            wcodes[c] = keep.tile([P, HALF], U32, name="wcodes%d" % c, align_bytes=256)
+            wscales[c] = keep.tile([P, HALF], U8, name="wscales%d" % c, align_bytes=256)
             nc.vector.quantize_mx(
                 out=wcodes[c][:].bitcast(E4X4),
                 scales=wscales[c][:],
@@ -105,16 +106,21 @@ def tile_virtual16bmatmul_t_kernel(tc, x, weight_upper, weight_lower, grad_out, 
                 out=grp[:].bitcast(F32).rearrange("p (g r u) -> p g r u", g=2, u=2),
                 in_=xt[:].rearrange("p (g u) r -> p g r u", u=2),
             )
-            gcodes[t] = keep.tile([P, 256], U32, name="gcodes%d" % t, align_bytes=64)
-            gscales[t] = keep.tile([P, 256], U8, name="gscales%d" % t, align_bytes=64)
-            nc.vector.quantize_mx(out=gcodes[t][:].bitcast(E5X4), scales=gscales[t][:], in_=grp[:])
+            gcodes[t] = keep.tile([P, PAD + 256], U32, name="gcodes%d" % t, align_bytes=256)
+            gscales[t] = keep.tile([P, 2, 256], U8, name="gscales%d" % t, align_bytes=256)
+            for g in range(2):
+                nc.vector.quantize_mx(
+                    out=gcodes[t][:, PAD + P * g : PAD + P * (g + 1)].bitcast(E5X4),
+                    scales=gscales[t][:, g, 0:P],
+                    in_=grp[:, 512 * g : 512 * (g + 1)],
+                )
 
         def mx_pass(acc, t, c):
             g = (c // 2) % 2
             nc.tensor.matmul_mx(
                 out=acc[:],
-                lhsT=gcodes[t][:, P * g : P * (g + 1)].bitcast(E5X4),
-                lhsT_scale=gscales[t][:, P * g : P * (g + 1)],
+                lhsT=gcodes[t][:, PAD + P * g : PAD + P * (g + 1)].bitcast(E5X4),
+                lhsT_scale=gscales[t][:, g, 0:P],
                 rhs=wcodes[c][:].bitcast(E4X4),
                 rhs_scale=wscales[c][:],
                 start=(c % 4 == 0),

@@ -15,7 +15,6 @@ E5X4 = mybir.dt.float8_e5m2_x4
 
 P = 128
 HALF = 512
-PAD = 48
 V_COLS = 336
 
 
@@ -34,8 +33,15 @@ def tile_virtual16bmatmul_t_kernel(tc, x, weight_upper, weight_lower, grad_out, 
         ggrp_pool = ctx.enter_context(tc.tile_pool(name="ggrp", bufs=4))
         psum = ctx.enter_context(tc.psum_pool(name="psum", bufs=1))
 
+        zeros = keep.tile([P, HALF], BF16, name="zeros")
+        nc.vector.memset(zeros[:], 0.0)
         ident = keep.tile([P, P], F32, name="ident")
         masks.make_identity(nc, ident[:])
+        idle = psum.tile([P, HALF], F32, name="idle", tag="bank7")
+
+        def warm(n):
+            for i in range(n):
+                nc.tensor.matmul(out=idle[:], lhsT=zeros[:, 0:P], rhs=zeros[:], start=True, stop=True)
 
         wraw = {}
         wgrp = {}
@@ -84,8 +90,8 @@ def tile_virtual16bmatmul_t_kernel(tc, x, weight_upper, weight_lower, grad_out, 
             regroup_w(c, nc.scalar.copy, V_COLS, HALF)
 
         def quantise_w(c):
-            wcodes[c] = keep.tile([P, HALF], U32, name="wcodes%d" % c, align_bytes=256)
-            wscales[c] = keep.tile([P, HALF], U8, name="wscales%d" % c, align_bytes=256)
+            wcodes[c] = keep.tile([P, HALF], U32, name="wcodes%d" % c, align_bytes=64)
+            wscales[c] = keep.tile([P, HALF], U8, name="wscales%d" % c, align_bytes=64)
             nc.vector.quantize_mx(
                 out=wcodes[c][:].bitcast(E4X4),
                 scales=wscales[c][:],
@@ -106,21 +112,16 @@ def tile_virtual16bmatmul_t_kernel(tc, x, weight_upper, weight_lower, grad_out, 
                 out=grp[:].bitcast(F32).rearrange("p (g r u) -> p g r u", g=2, u=2),
                 in_=xt[:].rearrange("p (g u) r -> p g r u", u=2),
             )
-            gcodes[t] = keep.tile([P, PAD + 256], U32, name="gcodes%d" % t, align_bytes=256)
-            gscales[t] = keep.tile([P, 2, 256], U8, name="gscales%d" % t, align_bytes=256)
-            for g in range(2):
-                nc.vector.quantize_mx(
-                    out=gcodes[t][:, PAD + P * g : PAD + P * (g + 1)].bitcast(E5X4),
-                    scales=gscales[t][:, g, 0:P],
-                    in_=grp[:, 512 * g : 512 * (g + 1)],
-                )
+            gcodes[t] = keep.tile([P, 256], U32, name="gcodes%d" % t, align_bytes=64)
+            gscales[t] = keep.tile([P, 256], U8, name="gscales%d" % t, align_bytes=64)
+            nc.vector.quantize_mx(out=gcodes[t][:].bitcast(E5X4), scales=gscales[t][:], in_=grp[:])
 
         def mx_pass(acc, t, c):
             g = (c // 2) % 2
             nc.tensor.matmul_mx(
                 out=acc[:],
-                lhsT=gcodes[t][:, PAD + P * g : PAD + P * (g + 1)].bitcast(E5X4),
-                lhsT_scale=gscales[t][:, g, 0:P],
+                lhsT=gcodes[t][:, P * g : P * (g + 1)].bitcast(E5X4),
+                lhsT_scale=gscales[t][:, P * g : P * (g + 1)],
                 rhs=wcodes[c][:].bitcast(E4X4),
                 rhs_scale=wscales[c][:],
                 start=(c % 4 == 0),
@@ -132,24 +133,54 @@ def tile_virtual16bmatmul_t_kernel(tc, x, weight_upper, weight_lower, grad_out, 
             copy(out=stage[:], in_=banks[t][:])
             nc.sync.dma_start(out=o_rows[P * t : P * (t + 1), HALF * h : HALF * (h + 1)], in_=stage[:])
 
+        load_g_early(0)
+        load_g_early(1)
         load_w(0)
-        for t in range(8):
+        for t in range(2, 6):
             load_g_early(t)
-        for c in range(1, 8):
+        load_w(1)
+        load_g_early(6)
+        load_g_early(7)
+        for c in range(2, 8):
             load_w(c)
         for i in range(2):
             load_g_late(i)
 
-        prepare_w(0)
-        for t in range(8):
-            prepare_g(t)
+        def open_a(t):
+            banks[t] = psum.tile([P, HALF], F32, name="accA%d" % t, tag="bank%d" % t)
 
-        for c in range(4):
-            prepare_w(c + 1)
-            for t in range(8):
-                if c == 0:
-                    banks[t] = psum.tile([P, HALF], F32, name="accA%d" % t, tag="bank%d" % t)
-                mx_pass(banks[t], t, c)
+        warm(8)
+        prepare_g(0)
+        prepare_g(1)
+        warm(3)
+        prepare_w(0)
+        prepare_g(2)
+        warm(1)
+        prepare_g(3)
+        warm(1)
+        prepare_g(4)
+        warm(1)
+        prepare_g(5)
+
+        for t in range(6):
+            open_a(t)
+            mx_pass(banks[t], t, 0)
+        prepare_w(1)
+        prepare_g(6)
+        prepare_g(7)
+        for t in range(6):
+            mx_pass(banks[t], t, 1)
+        for t in range(6, 8):
+            open_a(t)
+            mx_pass(banks[t], t, 0)
+            mx_pass(banks[t], t, 1)
+        prepare_w(2)
+        prepare_w(3)
+        for t in range(8):
+            mx_pass(banks[t], t, 2)
+        prepare_w(4)
+        for t in range(8):
+            mx_pass(banks[t], t, 3)
         prepare_w(5)
         empty_early(0, 0, nc.scalar.copy)
         empty_early(1, 0, nc.scalar.copy)

@@ -22,8 +22,9 @@ def tile_virtual16bmatmul_t_kernel(tc, x, weight_upper, weight_lower, grad_out, 
     nc = tc.nc
     g_rows = grad_out.flatten_outer_dims()
     o_rows = out.flatten_outer_dims()
-    g_late = g_rows[1024:2048, :].rearrange("(p j) k -> p j k", j=8)
-    o_late = o_rows[1024:2048, :].rearrange("(p j) n -> p j n", j=8)
+    g_mid = g_rows[1024:1536, :].rearrange("(p j) k -> p (j k)", j=4)
+    o_mid = o_rows[1024:1536, :].rearrange("(p j) n -> p j n", j=4)
+    g_last = g_rows[1536:2048, :].rearrange("(r j) k -> j r k", j=32)
     weights = (weight_upper, weight_lower)
 
     with ExitStack() as ctx:
@@ -69,11 +70,46 @@ def tile_virtual16bmatmul_t_kernel(tc, x, weight_upper, weight_lower, grad_out, 
             nc.sync.dma_start(out=raw[:], in_=g_rows[P * t : P * (t + 1), :])
             gwords[t] = raw[:].bitcast(F32)
 
-        def load_g_late(i):
-            raw = keep.tile([P, 4096], BF16, name="glate%d" % i)
-            nc.sync.dma_start(out=raw[:], in_=g_late[:, 4 * i : 4 * i + 4, :].rearrange("p j k -> p (j k)"))
+        def load_g_mid():
+            raw = keep.tile([P, 4096], BF16, name="gmid")
+            nc.sync.dma_start(out=raw[:], in_=g_mid)
             for jj in range(4):
-                gwords[8 + 4 * i + jj] = raw[:].bitcast(F32)[:, 512 * jj : 512 * (jj + 1)]
+                gwords[8 + jj] = raw[:].bitcast(F32)[:, 512 * jj : 512 * (jj + 1)]
+
+        gquad = keep.tile([P, 4096], BF16, name="gquad", align_bytes=64)
+        gturn = keep.tile([P, 2048], F32, name="gturn", align_bytes=64)
+        last_codes = {}
+        last_scales = {}
+
+        def load_g_last():
+            dst = gquad[:].rearrange("p (g r u w) -> p g r u w", g=2, u=2, w=64)
+            for g in range(2):
+                for u in range(2):
+                    for a in range(4):
+                        k0 = 512 * g + 256 * u + 64 * a
+                        nc.sync.dma_start(
+                            out=dst[32 * a : 32 * (a + 1), g, :, u, :],
+                            in_=g_last[:, :, k0 : k0 + 64],
+                        )
+
+        def turn_last(g):
+            nc.vector.transpose(
+                out=gturn[:, 1024 * g : 1024 * (g + 1)],
+                in_=gquad[:].bitcast(F32)[:, 1024 * g : 1024 * (g + 1)],
+            )
+
+        def group_last(g):
+            grp = keep.tile([P, 2048], BF16, name="lgrp%d" % g, align_bytes=64)
+            nc.scalar.copy(
+                out=grp[:].bitcast(F32).rearrange("p (r j u) -> p r j u", r=16, u=2),
+                in_=gturn[:, 1024 * g : 1024 * (g + 1)].rearrange("p (r u j) -> p r j u", r=16, u=2),
+            )
+            ggrp[g] = grp
+
+        def quantise_last(g):
+            last_codes[g] = keep.tile([P, HALF], U32, name="lcodes%d" % g, align_bytes=64)
+            last_scales[g] = keep.tile([P, HALF], U8, name="lscales%d" % g, align_bytes=64)
+            nc.vector.quantize_mx(out=last_codes[g][:].bitcast(E5X4), scales=last_scales[g][:], in_=ggrp[g][:])
 
         def regroup_w(c, copy, lo, hi):
             if c not in wgrp:
@@ -118,10 +154,16 @@ def tile_virtual16bmatmul_t_kernel(tc, x, weight_upper, weight_lower, grad_out, 
 
         def mx_pass(acc, t, c):
             g = (c // 2) % 2
+            if t < 12:
+                codes = gcodes[t][:, P * g : P * (g + 1)]
+                scales = gscales[t][:, P * g : P * (g + 1)]
+            else:
+                codes = last_codes[g][:, P * (t - 12) : P * (t - 11)]
+                scales = last_scales[g][:, P * (t - 12) : P * (t - 11)]
             nc.tensor.matmul_mx(
                 out=acc[:],
-                lhsT=gcodes[t][:, P * g : P * (g + 1)].bitcast(E5X4),
-                lhsT_scale=gscales[t][:, P * g : P * (g + 1)],
+                lhsT=codes.bitcast(E5X4),
+                lhsT_scale=scales,
                 rhs=wcodes[c][:].bitcast(E4X4),
                 rhs_scale=wscales[c][:],
                 start=(c % 4 == 0),
@@ -143,8 +185,8 @@ def tile_virtual16bmatmul_t_kernel(tc, x, weight_upper, weight_lower, grad_out, 
         load_g_early(7)
         for c in range(2, 8):
             load_w(c)
-        for i in range(2):
-            load_g_late(i)
+        load_g_mid()
+        load_g_last()
 
         def open_a(t):
             banks[t] = psum.tile([P, HALF], F32, name="accA%d" % t, tag="bank%d" % t)
@@ -204,7 +246,7 @@ def tile_virtual16bmatmul_t_kernel(tc, x, weight_upper, weight_lower, grad_out, 
         for t in range(8):
             empty_early(t, 1, nc.scalar.copy if t % 2 == 0 else nc.vector.tensor_copy)
 
-        for t in range(8, 16):
+        for t in range(8, 12):
             prepare_g(t)
         for t in range(8, 16):
             stage = keep.tile([P, 2 * HALF], F32, name="o%d" % t)
@@ -217,7 +259,19 @@ def tile_virtual16bmatmul_t_kernel(tc, x, weight_upper, weight_lower, grad_out, 
                 copy(out=stage[:, HALF * h : HALF * (h + 1)], in_=acc[:])
                 if t == 15:
                     nc.sync.dma_start(
-                        out=o_late[:, t - 8, HALF * h : HALF * (h + 1)], in_=stage[:, HALF * h : HALF * (h + 1)]
+                        out=o_rows[P * t : P * (t + 1), HALF * h : HALF * (h + 1)],
+                        in_=stage[:, HALF * h : HALF * (h + 1)],
                     )
-            if t < 15:
-                nc.sync.dma_start(out=o_late[:, t - 8, :], in_=stage[:])
+            if t < 12:
+                nc.sync.dma_start(out=o_mid[:, t - 8, :], in_=stage[:])
+            elif t < 15:
+                nc.sync.dma_start(out=o_rows[P * t : P * (t + 1), :], in_=stage[:])
+            if t == 8:
+                turn_last(0)
+                turn_last(1)
+                group_last(0)
+            if t == 9:
+                quantise_last(0)
+                group_last(1)
+            if t == 10:
+                quantise_last(1)

@@ -22,9 +22,7 @@ def tile_virtual16bmatmul_t_kernel(tc, x, weight_upper, weight_lower, grad_out, 
     nc = tc.nc
     g_rows = grad_out.flatten_outer_dims()
     o_rows = out.flatten_outer_dims()
-    g_mid = g_rows[1024:1536, :].rearrange("(p j) k -> p (j k)", j=4)
-    o_mid = o_rows[1024:1536, :].rearrange("(p j) n -> p j n", j=4)
-    g_last = g_rows[1536:2048, :].rearrange("(r j) k -> j r k", j=32)
+    g_late = g_rows[1024:2048, :].rearrange("(q r j) k -> q j r k", q=2, j=32)
     weights = (weight_upper, weight_lower)
 
     with ExitStack() as ctx:
@@ -53,6 +51,7 @@ def tile_virtual16bmatmul_t_kernel(tc, x, weight_upper, weight_lower, grad_out, 
         gcodes = {}
         gscales = {}
         banks = {}
+        stages = {}
 
         def load_w(c):
             h, g, w = c // 4, (c // 2) % 2, c % 2
@@ -70,46 +69,41 @@ def tile_virtual16bmatmul_t_kernel(tc, x, weight_upper, weight_lower, grad_out, 
             nc.sync.dma_start(out=raw[:], in_=g_rows[P * t : P * (t + 1), :])
             gwords[t] = raw[:].bitcast(F32)
 
-        def load_g_mid():
-            raw = keep.tile([P, 4096], BF16, name="gmid")
-            nc.sync.dma_start(out=raw[:], in_=g_mid)
-            for jj in range(4):
-                gwords[8 + jj] = raw[:].bitcast(F32)[:, 512 * jj : 512 * (jj + 1)]
+        gquad = {}
+        gturn = {}
+        for q in range(2):
+            gquad[q] = keep.tile([P, 4096], BF16, name="gquad%d" % q, align_bytes=64)
+            gturn[q] = keep.tile([P, 2048], F32, name="gturn%d" % q, align_bytes=64)
 
-        gquad = keep.tile([P, 4096], BF16, name="gquad", align_bytes=64)
-        gturn = keep.tile([P, 2048], F32, name="gturn", align_bytes=64)
-        last_codes = {}
-        last_scales = {}
-
-        def load_g_last():
-            dst = gquad[:].rearrange("p (g r u w) -> p g r u w", g=2, u=2, w=64)
+        def load_quad(q):
+            dst = gquad[q][:].rearrange("p (g r u w) -> p g r u w", g=2, u=2, w=64)
             for g in range(2):
                 for u in range(2):
                     for a in range(4):
                         k0 = 512 * g + 256 * u + 64 * a
                         nc.sync.dma_start(
                             out=dst[32 * a : 32 * (a + 1), g, :, u, :],
-                            in_=g_last[:, :, k0 : k0 + 64],
+                            in_=g_late[q, :, :, k0 : k0 + 64],
                         )
 
-        def turn_last(g):
+        def turn_quad(q, g):
             nc.vector.transpose(
-                out=gturn[:, 1024 * g : 1024 * (g + 1)],
-                in_=gquad[:].bitcast(F32)[:, 1024 * g : 1024 * (g + 1)],
+                out=gturn[q][:, 1024 * g : 1024 * (g + 1)],
+                in_=gquad[q][:].bitcast(F32)[:, 1024 * g : 1024 * (g + 1)],
             )
 
-        def group_last(g):
-            grp = keep.tile([P, 2048], BF16, name="lgrp%d" % g, align_bytes=64)
-            nc.scalar.copy(
+        def group_quad(q, g, copy):
+            grp = keep.tile([P, 2048], BF16, name="qgrp%d_%d" % (q, g), align_bytes=64)
+            copy(
                 out=grp[:].bitcast(F32).rearrange("p (r j u) -> p r j u", r=16, u=2),
-                in_=gturn[:, 1024 * g : 1024 * (g + 1)].rearrange("p (r u j) -> p r j u", r=16, u=2),
+                in_=gturn[q][:, 1024 * g : 1024 * (g + 1)].rearrange("p (r u j) -> p r j u", r=16, u=2),
             )
-            ggrp[g] = grp
+            ggrp[q, g] = grp
 
-        def quantise_last(g):
-            last_codes[g] = keep.tile([P, HALF], U32, name="lcodes%d" % g, align_bytes=64)
-            last_scales[g] = keep.tile([P, HALF], U8, name="lscales%d" % g, align_bytes=64)
-            nc.vector.quantize_mx(out=last_codes[g][:].bitcast(E5X4), scales=last_scales[g][:], in_=ggrp[g][:])
+        def quantise_quad(q, g):
+            gcodes[q, g] = keep.tile([P, HALF], U32, name="qcodes%d_%d" % (q, g), align_bytes=64)
+            gscales[q, g] = keep.tile([P, HALF], U8, name="qscales%d_%d" % (q, g), align_bytes=64)
+            nc.vector.quantize_mx(out=gcodes[q, g][:].bitcast(E5X4), scales=gscales[q, g][:], in_=ggrp[q, g][:])
 
         def regroup_w(c, copy, lo, hi):
             if c not in wgrp:
@@ -154,12 +148,13 @@ def tile_virtual16bmatmul_t_kernel(tc, x, weight_upper, weight_lower, grad_out, 
 
         def mx_pass(acc, t, c):
             g = (c // 2) % 2
-            if t < 12:
+            if t < 8:
                 codes = gcodes[t][:, P * g : P * (g + 1)]
                 scales = gscales[t][:, P * g : P * (g + 1)]
             else:
-                codes = last_codes[g][:, P * (t - 12) : P * (t - 11)]
-                scales = last_scales[g][:, P * (t - 12) : P * (t - 11)]
+                q, i = t // 4 - 2, t % 4
+                codes = gcodes[q, g][:, P * i : P * (i + 1)]
+                scales = gscales[q, g][:, P * i : P * (i + 1)]
             nc.tensor.matmul_mx(
                 out=acc[:],
                 lhsT=codes.bitcast(E5X4),
@@ -171,9 +166,11 @@ def tile_virtual16bmatmul_t_kernel(tc, x, weight_upper, weight_lower, grad_out, 
             )
 
         def empty_early(t, h, copy):
-            stage = keep.tile([P, HALF], F32, name="o%d_%d" % (t, h))
-            copy(out=stage[:], in_=banks[t][:])
-            nc.sync.dma_start(out=o_rows[P * t : P * (t + 1), HALF * h : HALF * (h + 1)], in_=stage[:])
+            if h == 0:
+                stages[t] = keep.tile([P, 2 * HALF], F32, name="o%d" % t)
+            copy(out=stages[t][:, HALF * h : HALF * (h + 1)], in_=banks[t][:])
+            if h == 1:
+                nc.sync.dma_start(out=o_rows[P * t : P * (t + 1), :], in_=stages[t][:])
 
         load_g_early(0)
         load_g_early(1)
@@ -185,8 +182,8 @@ def tile_virtual16bmatmul_t_kernel(tc, x, weight_upper, weight_lower, grad_out, 
         load_g_early(7)
         for c in range(2, 8):
             load_w(c)
-        load_g_mid()
-        load_g_last()
+        for q in range(2):
+            load_quad(q)
 
         def open_a(t):
             banks[t] = psum.tile([P, HALF], F32, name="accA%d" % t, tag="bank%d" % t)
@@ -243,11 +240,20 @@ def tile_virtual16bmatmul_t_kernel(tc, x, weight_upper, weight_lower, grad_out, 
                     banks[t] = psum.tile([P, HALF], F32, name="accB%d" % t, tag="bank%d" % t)
                 mx_pass(banks[t], t, first)
                 mx_pass(banks[t], t, first + 1)
-        for t in range(8):
+        def empty_b(t):
             empty_early(t, 1, nc.scalar.copy if t % 2 == 0 else nc.vector.tensor_copy)
 
-        for t in range(8, 12):
-            prepare_g(t)
+        turn_quad(0, 0)
+        group_quad(0, 0, nc.scalar.copy)
+        turn_quad(0, 1)
+        quantise_quad(0, 0)
+        group_quad(0, 1, nc.vector.tensor_copy)
+        empty_b(0)
+        empty_b(1)
+        quantise_quad(0, 1)
+        for t in range(2, 8):
+            empty_b(t)
+
         for t in range(8, 16):
             stage = keep.tile([P, 2 * HALF], F32, name="o%d" % t)
             for h in range(2):
@@ -262,16 +268,14 @@ def tile_virtual16bmatmul_t_kernel(tc, x, weight_upper, weight_lower, grad_out, 
                         out=o_rows[P * t : P * (t + 1), HALF * h : HALF * (h + 1)],
                         in_=stage[:, HALF * h : HALF * (h + 1)],
                     )
-            if t < 12:
-                nc.sync.dma_start(out=o_mid[:, t - 8, :], in_=stage[:])
-            elif t < 15:
+            if t < 15:
                 nc.sync.dma_start(out=o_rows[P * t : P * (t + 1), :], in_=stage[:])
             if t == 8:
-                turn_last(0)
-                turn_last(1)
-                group_last(0)
+                turn_quad(1, 0)
+                group_quad(1, 0, nc.scalar.copy)
+                turn_quad(1, 1)
             if t == 9:
-                quantise_last(0)
-                group_last(1)
+                quantise_quad(1, 0)
+                group_quad(1, 1, nc.scalar.copy)
             if t == 10:
-                quantise_last(1)
+                quantise_quad(1, 1)

@@ -48,6 +48,7 @@ def tile_virtual16bmatmul_t_kernel(tc, x, weight_upper, weight_lower, grad_out, 
         wscales = {}
         gwords = {}
         ggrp = {}
+        xt = {}
         gcodes = {}
         gscales = {}
         banks = {}
@@ -128,23 +129,28 @@ def tile_virtual16bmatmul_t_kernel(tc, x, weight_upper, weight_lower, grad_out, 
                 in_=wgrp[c][:].rearrange("p c t -> p (c t)"),
             )
 
-        def prepare_w(c):
-            regroup_w_vector(c)
+        def regroup_w_both(c):
             regroup_w_scalar(c)
-            quantise_w(c)
+            regroup_w_vector(c)
 
-        def prepare_g(t):
-            xt = psum.tile([P, 4, P], F32, name="xt%d" % t, tag="bank%d" % (t % 8))
+        def transpose_g(t):
+            xt[t] = psum.tile([P, 4, P], F32, name="xt%d" % t, tag="bank%d" % t)
             for j in range(4):
-                nc.tensor.transpose(xt[:, j, :], gwords[t][:, P * j : P * (j + 1)], ident[:])
+                nc.tensor.transpose(xt[t][:, j, :], gwords[t][:, P * j : P * (j + 1)], ident[:])
+
+        def quantise_g(t):
             grp = ggrp_pool.tile([P, 1024], BF16, name="ggrp%d" % t, tag="ggrp", align_bytes=64)
             nc.scalar.copy(
                 out=grp[:].bitcast(F32).rearrange("p (g r u) -> p g r u", g=2, u=2),
-                in_=xt[:].rearrange("p (g u) r -> p g r u", u=2),
+                in_=xt[t][:].rearrange("p (g u) r -> p g r u", u=2),
             )
             gcodes[t] = keep.tile([P, 256], U32, name="gcodes%d" % t, align_bytes=64)
             gscales[t] = keep.tile([P, 256], U8, name="gscales%d" % t, align_bytes=64)
             nc.vector.quantize_mx(out=gcodes[t][:].bitcast(E5X4), scales=gscales[t][:], in_=grp[:])
+
+        def prepare_g(t):
+            transpose_g(t)
+            quantise_g(t)
 
         def mx_pass(acc, t, c):
             g = (c // 2) % 2
@@ -188,51 +194,59 @@ def tile_virtual16bmatmul_t_kernel(tc, x, weight_upper, weight_lower, grad_out, 
         def open_a(t):
             banks[t] = psum.tile([P, HALF], F32, name="accA%d" % t, tag="bank%d" % t)
 
-        warm(8)
+        warm(4)
         prepare_g(0)
+        warm(1)
         prepare_g(1)
         warm(3)
-        prepare_w(0)
+        regroup_w_both(0)
+        quantise_w(0)
         prepare_g(2)
-        warm(1)
-        prepare_g(3)
-        warm(1)
-        prepare_g(4)
-        warm(1)
-        prepare_g(5)
+        for t in range(3, 6):
+            warm(1)
+            prepare_g(t)
 
         for t in range(6):
             open_a(t)
             mx_pass(banks[t], t, 0)
-        prepare_w(1)
-        prepare_g(6)
-        prepare_g(7)
+        regroup_w_both(1)
+        transpose_g(6)
+        warm(2)
+        transpose_g(7)
+        quantise_g(6)
+        quantise_w(1)
+        quantise_g(7)
         for t in range(6):
             mx_pass(banks[t], t, 1)
         for t in range(6, 8):
             open_a(t)
             mx_pass(banks[t], t, 0)
             mx_pass(banks[t], t, 1)
-        prepare_w(2)
-        prepare_w(3)
-        for t in range(8):
-            mx_pass(banks[t], t, 2)
-        prepare_w(4)
-        for t in range(8):
-            mx_pass(banks[t], t, 3)
-        prepare_w(5)
+        regroup_w_both(2)
+        regroup_w_both(3)
+        quantise_w(2)
+        quantise_w(3)
+        for c in (2, 3):
+            for t in range(8):
+                mx_pass(banks[t], t, c)
+        regroup_w_both(4)
+        regroup_w_both(5)
+        quantise_w(4)
         empty_early(0, 0, nc.scalar.copy)
+        regroup_w_vector(6)
+        quantise_w(5)
         empty_early(1, 0, nc.scalar.copy)
-        prepare_w(6)
         empty_early(2, 0, nc.scalar.copy)
-        empty_early(3, 0, nc.scalar.copy)
-        empty_early(4, 0, nc.vector.tensor_copy)
+        empty_early(3, 0, nc.vector.tensor_copy)
+        regroup_w_scalar(6)
+        empty_early(4, 0, nc.scalar.copy)
         regroup_w_vector(7)
+        quantise_w(6)
+        empty_early(5, 0, nc.vector.tensor_copy)
         regroup_w_scalar(7)
-        empty_early(5, 0, nc.scalar.copy)
-        empty_early(6, 0, nc.vector.tensor_copy)
-        empty_early(7, 0, nc.scalar.copy)
+        empty_early(6, 0, nc.scalar.copy)
         quantise_w(7)
+        empty_early(7, 0, nc.scalar.copy)
 
         for first in (4, 6):
             for t in range(8):

@@ -15,13 +15,15 @@ E5X4 = mybir.dt.float8_e5m2_x4
 
 P = 128
 HALF = 512
-V_COLS = 336
+V_COLS = 320
 
 
 def tile_virtual16bmatmul_t_kernel(tc, x, weight_upper, weight_lower, grad_out, out):
     nc = tc.nc
     g_rows = grad_out.flatten_outer_dims()
     o_rows = out.flatten_outer_dims()
+    g_early = g_rows[0:1024, :].rearrange("(p j) k -> p j k", j=8)
+    o_early = o_rows[0:1024, :].rearrange("(p j) n -> p j n", j=8)
     g_late = g_rows[1024:2048, :].rearrange("(q r j) k -> q j r k", q=2, j=32)
     weights = (weight_upper, weight_lower)
 
@@ -54,21 +56,30 @@ def tile_virtual16bmatmul_t_kernel(tc, x, weight_upper, weight_lower, grad_out, 
         banks = {}
         stages = {}
 
-        def load_w(c):
-            h, g, w = c // 4, (c // 2) % 2, c % 2
-            raw = keep.tile([P, 4, HALF], BF16, name="wraw%d" % c)
+        def load_rows(name, w, g, lo, hi):
+            raw = keep.tile([P, 4, hi - lo], BF16, name=name)
             for u in range(2):
                 r0 = 512 * g + 256 * u
                 nc.sync.dma_start(
                     out=raw[:, 2 * u : 2 * u + 2, :],
-                    in_=weights[w][r0 : r0 + 256, HALF * h : HALF * (h + 1)].rearrange("(p e) c -> p e c", e=2),
+                    in_=weights[w][r0 : r0 + 256, lo:hi].rearrange("(p e) c -> p e c", e=2),
                 )
-            wraw[c] = raw
+            return raw
 
-        def load_g_early(t):
-            raw = keep.tile([P, 1024], BF16, name="graw%d" % t)
-            nc.sync.dma_start(out=raw[:], in_=g_rows[P * t : P * (t + 1), :])
-            gwords[t] = raw[:].bitcast(F32)
+        def load_w(c):
+            h, g, w = c // 4, (c // 2) % 2, c % 2
+            wraw[c] = load_rows("wraw%d" % c, w, g, HALF * h, HALF * (h + 1))[:]
+
+        def load_w_whole(c):
+            raw = load_rows("wraw%d" % c, c % 2, c // 2, 0, 2 * HALF)
+            wraw[c] = raw[:, :, 0:HALF]
+            wraw[c + 4] = raw[:, :, HALF : 2 * HALF]
+
+        def load_g_early(t, n=1):
+            raw = keep.tile([P, n, 1024], BF16, name="graw%d" % t)
+            nc.sync.dma_start(out=raw[:], in_=g_early[:, t : t + n, :])
+            for i in range(n):
+                gwords[t + i] = raw[:, i, :].bitcast(F32)
 
         gquad = {}
         gturn = {}
@@ -172,21 +183,22 @@ def tile_virtual16bmatmul_t_kernel(tc, x, weight_upper, weight_lower, grad_out, 
             )
 
         def empty_early(t, h, copy):
-            if h == 0:
-                stages[t] = keep.tile([P, 2 * HALF], F32, name="o%d" % t)
-            copy(out=stages[t][:, HALF * h : HALF * (h + 1)], in_=banks[t][:])
-            if h == 1:
-                nc.sync.dma_start(out=o_rows[P * t : P * (t + 1), :], in_=stages[t][:])
+            if t % 4 == 0 and h == 0:
+                stages[t // 4] = keep.tile([P, 4, 2 * HALF], F32, name="o%d" % t)
+            copy(out=stages[t // 4][:, t % 4, HALF * h : HALF * (h + 1)], in_=banks[t][:])
+            if t % 4 == 3 and h == 1:
+                nc.sync.dma_start(out=o_early[:, t - 3 : t + 1, :], in_=stages[t // 4][:])
 
-        load_g_early(0)
-        load_g_early(1)
+        for t in range(3):
+            load_g_early(t)
         load_w(0)
-        for t in range(2, 6):
+        for t in range(3, 6):
             load_g_early(t)
         load_w(1)
-        load_g_early(6)
-        load_g_early(7)
-        for c in range(2, 8):
+        load_g_early(6, 2)
+        load_w(2)
+        load_w_whole(3)
+        for c in range(4, 7):
             load_w(c)
         for q in range(2):
             load_quad(q)
@@ -195,65 +207,62 @@ def tile_virtual16bmatmul_t_kernel(tc, x, weight_upper, weight_lower, grad_out, 
             banks[t] = psum.tile([P, HALF], F32, name="accA%d" % t, tag="bank%d" % t)
 
         warm(4)
-        prepare_g(0)
-        warm(1)
-        prepare_g(1)
-        warm(3)
+        for t in range(3):
+            prepare_g(t)
+            warm(1 if t < 2 else 4)
         regroup_w_both(0)
         quantise_w(0)
-        prepare_g(2)
         for t in range(3, 6):
-            warm(1)
             prepare_g(t)
+            if t < 5:
+                warm(1)
 
         for t in range(6):
             open_a(t)
             mx_pass(banks[t], t, 0)
         regroup_w_both(1)
-        transpose_g(6)
-        warm(2)
-        transpose_g(7)
-        quantise_g(6)
         quantise_w(1)
-        quantise_g(7)
+        prepare_g(6)
+        prepare_g(7)
         for t in range(6):
             mx_pass(banks[t], t, 1)
         for t in range(6, 8):
             open_a(t)
             mx_pass(banks[t], t, 0)
             mx_pass(banks[t], t, 1)
-        regroup_w_both(2)
-        regroup_w_both(3)
-        quantise_w(2)
-        quantise_w(3)
+        for c in (2, 3):
+            regroup_w_both(c)
+            quantise_w(c)
         for c in (2, 3):
             for t in range(8):
                 mx_pass(banks[t], t, c)
         regroup_w_both(4)
         regroup_w_both(5)
         quantise_w(4)
-        empty_early(0, 0, nc.scalar.copy)
         regroup_w_vector(6)
         quantise_w(5)
-        empty_early(1, 0, nc.scalar.copy)
-        empty_early(2, 0, nc.scalar.copy)
-        empty_early(3, 0, nc.vector.tensor_copy)
+        for t in range(4):
+            empty_early(t, 0, nc.scalar.copy)
+        empty_early(4, 0, nc.vector.tensor_copy)
+        empty_early(5, 0, nc.scalar.copy)
         regroup_w_scalar(6)
-        empty_early(4, 0, nc.scalar.copy)
+        empty_early(6, 0, nc.vector.tensor_copy)
         regroup_w_vector(7)
-        quantise_w(6)
-        empty_early(5, 0, nc.vector.tensor_copy)
-        regroup_w_scalar(7)
-        empty_early(6, 0, nc.scalar.copy)
-        quantise_w(7)
         empty_early(7, 0, nc.scalar.copy)
+        regroup_w_scalar(7)
+        quantise_w(6)
+        quantise_w(7)
 
-        for first in (4, 6):
-            for t in range(8):
-                if first == 4:
-                    banks[t] = psum.tile([P, HALF], F32, name="accB%d" % t, tag="bank%d" % t)
-                mx_pass(banks[t], t, first)
-                mx_pass(banks[t], t, first + 1)
+        for t0 in (0, 4):
+            for c in (4, 5):
+                for t in range(t0, t0 + 4):
+                    if c == 4:
+                        banks[t] = psum.tile([P, HALF], F32, name="accB%d" % t, tag="bank%d" % t)
+                    mx_pass(banks[t], t, c)
+        for t in range(8):
+            for c in (6, 7):
+                mx_pass(banks[t], t, c)
+
         def empty_b(t):
             empty_early(t, 1, nc.scalar.copy if t % 2 == 0 else nc.vector.tensor_copy)
 

from contextlib import ExitStack

import concourse.masks as masks
import concourse.mybir as mybir

FLOPS = 2 * 2 * 2048 * 1024 * 1024
BYTES = 2048 * 1024 * 2 + 2 * 1024 * 1024 * 2 + 2048 * 1024 * 4

F32 = mybir.dt.float32
BF16 = mybir.dt.bfloat16
U32 = mybir.dt.uint32
U8 = mybir.dt.uint8
E4X4 = mybir.dt.float8_e4m3fn_x4
E5X4 = mybir.dt.float8_e5m2_x4

P = 128
HALF = 512
V_COLS = 320


def tile_virtual16bmatmul_t_kernel(tc, x, weight_upper, weight_lower, grad_out, out):
    nc = tc.nc
    g_rows = grad_out.flatten_outer_dims()
    o_rows = out.flatten_outer_dims()
    g_early = g_rows[0:1024, :].rearrange("(p j) k -> p j k", j=8)
    o_early = o_rows[0:1024, :].rearrange("(p j) n -> p j n", j=8)
    g_late = g_rows[1024:2048, :].rearrange("(q r j) k -> q j r k", q=2, j=32)
    weights = (weight_upper, weight_lower)

    with ExitStack() as ctx:
        ctx.enter_context(tc.manual_schedule())
        keep = ctx.enter_context(tc.tile_pool(name="keep", bufs=1))
        wgrp_pool = ctx.enter_context(tc.tile_pool(name="wgrp", bufs=3))
        ggrp_pool = ctx.enter_context(tc.tile_pool(name="ggrp", bufs=4))
        psum = ctx.enter_context(tc.psum_pool(name="psum", bufs=1))

        zeros = keep.tile([P, HALF], BF16, name="zeros")
        nc.vector.memset(zeros[:], 0.0)
        ident = keep.tile([P, P], F32, name="ident")
        masks.make_identity(nc, ident[:])
        idle = psum.tile([P, HALF], F32, name="idle", tag="bank7")

        def warm(n):
            for i in range(n):
                nc.tensor.matmul(out=idle[:], lhsT=zeros[:, 0:P], rhs=zeros[:], start=True, stop=True)

        wraw = {}
        wgrp = {}
        wcodes = {}
        wscales = {}
        gwords = {}
        ggrp = {}
        xt = {}
        gcodes = {}
        gscales = {}
        banks = {}
        stages = {}

        def load_rows(name, w, g, lo, hi):
            raw = keep.tile([P, 4, hi - lo], BF16, name=name)
            for u in range(2):
                r0 = 512 * g + 256 * u
                nc.sync.dma_start(
                    out=raw[:, 2 * u : 2 * u + 2, :],
                    in_=weights[w][r0 : r0 + 256, lo:hi].rearrange("(p e) c -> p e c", e=2),
                )
            return raw

        def load_w(c):
            h, g, w = c // 4, (c // 2) % 2, c % 2
            wraw[c] = load_rows("wraw%d" % c, w, g, HALF * h, HALF * (h + 1))[:]

        def load_w_whole(c):
            raw = load_rows("wraw%d" % c, c % 2, c // 2, 0, 2 * HALF)
            wraw[c] = raw[:, :, 0:HALF]
            wraw[c + 4] = raw[:, :, HALF : 2 * HALF]

        def load_g_early(t, n=1):
            raw = keep.tile([P, n, 1024], BF16, name="graw%d" % t)
            nc.sync.dma_start(out=raw[:], in_=g_early[:, t : t + n, :])
            for i in range(n):
                gwords[t + i] = raw[:, i, :].bitcast(F32)

        gquad = {}
        gturn = {}
        for q in range(2):
            gquad[q] = keep.tile([P, 4096], BF16, name="gquad%d" % q, align_bytes=64)
            gturn[q] = keep.tile([P, 2048], F32, name="gturn%d" % q, align_bytes=64)

        def load_quad(q):
            dst = gquad[q][:].rearrange("p (g r u w) -> p g r u w", g=2, u=2, w=64)
            for g in range(2):
                for u in range(2):
                    for a in range(4):
                        k0 = 512 * g + 256 * u + 64 * a
                        nc.sync.dma_start(
                            out=dst[32 * a : 32 * (a + 1), g, :, u, :],
                            in_=g_late[q, :, :, k0 : k0 + 64],
                        )

        def turn_quad(q, g):
            nc.vector.transpose(
                out=gturn[q][:, 1024 * g : 1024 * (g + 1)],
                in_=gquad[q][:].bitcast(F32)[:, 1024 * g : 1024 * (g + 1)],
            )

        def group_quad(q, g, copy):
            grp = keep.tile([P, 2048], BF16, name="qgrp%d_%d" % (q, g), align_bytes=64)
            copy(
                out=grp[:].bitcast(F32).rearrange("p (r j u) -> p r j u", r=16, u=2),
                in_=gturn[q][:, 1024 * g : 1024 * (g + 1)].rearrange("p (r u j) -> p r j u", r=16, u=2),
            )
            ggrp[q, g] = grp

        def quantise_quad(q, g):
            gcodes[q, g] = keep.tile([P, HALF], U32, name="qcodes%d_%d" % (q, g), align_bytes=64)
            gscales[q, g] = keep.tile([P, HALF], U8, name="qscales%d_%d" % (q, g), align_bytes=64)
            nc.vector.quantize_mx(out=gcodes[q, g][:].bitcast(E5X4), scales=gscales[q, g][:], in_=ggrp[q, g][:])

        def regroup_w(c, copy, lo, hi):
            if c not in wgrp:
                wgrp[c] = wgrp_pool.tile([P, HALF, 4], BF16, name="wgrp%d" % c, tag="wgrp", align_bytes=64)
            copy(
                out=wgrp[c][:, lo:hi, :].rearrange("p (c i) t -> p c t i", i=4),
                in_=wraw[c][:, :, lo:hi].rearrange("p t (c i) -> p c t i", i=4),
            )

        def regroup_w_vector(c):
            regroup_w(c, nc.vector.tensor_copy, 0, V_COLS)

        def regroup_w_scalar(c):
            regroup_w(c, nc.scalar.copy, V_COLS, HALF)

        def quantise_w(c):
            wcodes[c] = keep.tile([P, HALF], U32, name="wcodes%d" % c, align_bytes=64)
            wscales[c] = keep.tile([P, HALF], U8, name="wscales%d" % c, align_bytes=64)
            nc.vector.quantize_mx(
                out=wcodes[c][:].bitcast(E4X4),
                scales=wscales[c][:],
                in_=wgrp[c][:].rearrange("p c t -> p (c t)"),
            )

        def regroup_w_both(c):
            regroup_w_scalar(c)
            regroup_w_vector(c)

        def transpose_g(t):
            xt[t] = psum.tile([P, 4, P], F32, name="xt%d" % t, tag="bank%d" % t)
            for j in range(4):
                nc.tensor.transpose(xt[t][:, j, :], gwords[t][:, P * j : P * (j + 1)], ident[:])

        def quantise_g(t):
            grp = ggrp_pool.tile([P, 1024], BF16, name="ggrp%d" % t, tag="ggrp", align_bytes=64)
            nc.scalar.copy(
                out=grp[:].bitcast(F32).rearrange("p (g r u) -> p g r u", g=2, u=2),
                in_=xt[t][:].rearrange("p (g u) r -> p g r u", u=2),
            )
            gcodes[t] = keep.tile([P, 256], U32, name="gcodes%d" % t, align_bytes=64)
            gscales[t] = keep.tile([P, 256], U8, name="gscales%d" % t, align_bytes=64)
            nc.vector.quantize_mx(out=gcodes[t][:].bitcast(E5X4), scales=gscales[t][:], in_=grp[:])

        def prepare_g(t):
            transpose_g(t)
            quantise_g(t)

        def mx_pass(acc, t, c):
            g = (c // 2) % 2
            if t < 8:
                codes = gcodes[t][:, P * g : P * (g + 1)]
                scales = gscales[t][:, P * g : P * (g + 1)]
            else:
                q, i = t // 4 - 2, t % 4
                codes = gcodes[q, g][:, P * i : P * (i + 1)]
                scales = gscales[q, g][:, P * i : P * (i + 1)]
            nc.tensor.matmul_mx(
                out=acc[:],
                lhsT=codes.bitcast(E5X4),
                lhsT_scale=scales,
                rhs=wcodes[c][:].bitcast(E4X4),
                rhs_scale=wscales[c][:],
                start=(c % 4 == 0),
                stop=(c % 4 == 3),
            )

        def empty_early(t, h, copy):
            if t % 4 == 0 and h == 0:
                stages[t // 4] = keep.tile([P, 4, 2 * HALF], F32, name="o%d" % t)
            copy(out=stages[t // 4][:, t % 4, HALF * h : HALF * (h + 1)], in_=banks[t][:])
            if t % 4 == 3 and h == 1:
                nc.sync.dma_start(out=o_early[:, t - 3 : t + 1, :], in_=stages[t // 4][:])

        for t in range(3):
            load_g_early(t)
        load_w(0)
        for t in range(3, 6):
            load_g_early(t)
        load_w(1)
        load_g_early(6, 2)
        load_w(2)
        load_w_whole(3)
        for c in range(4, 7):
            load_w(c)
        for q in range(2):
            load_quad(q)

        def open_a(t):
            banks[t] = psum.tile([P, HALF], F32, name="accA%d" % t, tag="bank%d" % t)

        warm(4)
        for t in range(3):
            prepare_g(t)
            warm(1 if t < 2 else 4)
        regroup_w_both(0)
        quantise_w(0)
        for t in range(3, 6):
            prepare_g(t)
            if t < 5:
                warm(1)

        for t in range(6):
            open_a(t)
            mx_pass(banks[t], t, 0)
        regroup_w_both(1)
        quantise_w(1)
        prepare_g(6)
        prepare_g(7)
        for t in range(6):
            mx_pass(banks[t], t, 1)
        for t in range(6, 8):
            open_a(t)
            mx_pass(banks[t], t, 0)
            mx_pass(banks[t], t, 1)
        for c in (2, 3):
            regroup_w_both(c)
            quantise_w(c)
        for c in (2, 3):
            for t in range(8):
                mx_pass(banks[t], t, c)
        regroup_w_both(4)
        regroup_w_both(5)
        quantise_w(4)
        regroup_w_vector(6)
        quantise_w(5)
        for t in range(4):
            empty_early(t, 0, nc.scalar.copy)
        empty_early(4, 0, nc.vector.tensor_copy)
        empty_early(5, 0, nc.scalar.copy)
        regroup_w_scalar(6)
        empty_early(6, 0, nc.vector.tensor_copy)
        regroup_w_vector(7)
        empty_early(7, 0, nc.scalar.copy)
        regroup_w_scalar(7)
        quantise_w(6)
        quantise_w(7)

        for t0 in (0, 4):
            for c in (4, 5):
                for t in range(t0, t0 + 4):
                    if c == 4:
                        banks[t] = psum.tile([P, HALF], F32, name="accB%d" % t, tag="bank%d" % t)
                    mx_pass(banks[t], t, c)
        for t in range(8):
            for c in (6, 7):
                mx_pass(banks[t], t, c)

        def empty_b(t):
            empty_early(t, 1, nc.scalar.copy if t % 2 == 0 else nc.vector.tensor_copy)

        turn_quad(0, 0)
        group_quad(0, 0, nc.scalar.copy)
        turn_quad(0, 1)
        quantise_quad(0, 0)
        group_quad(0, 1, nc.vector.tensor_copy)
        empty_b(0)
        empty_b(1)
        quantise_quad(0, 1)
        for t in range(2, 8):
            empty_b(t)

        for t in range(8, 16):
            stage = keep.tile([P, 2 * HALF], F32, name="o%d" % t)
            for h in range(2):
                q = 2 * (t - 8) + h
                acc = psum.tile([P, HALF], F32, name="accC%d" % q, tag="bank%d" % (q % 8))
                for c in range(4 * h, 4 * h + 4):
                    mx_pass(acc, t, c)
                copy = nc.scalar.copy if h == 0 else nc.vector.tensor_copy
                copy(out=stage[:, HALF * h : HALF * (h + 1)], in_=acc[:])
                if t == 15:
                    nc.sync.dma_start(
                        out=o_rows[P * t : P * (t + 1), HALF * h : HALF * (h + 1)],
                        in_=stage[:, HALF * h : HALF * (h + 1)],
                    )
            if t < 15:
                nc.sync.dma_start(out=o_rows[P * t : P * (t + 1), :], in_=stage[:])
            if t == 8:
                turn_quad(1, 0)
                group_quad(1, 0, nc.scalar.copy)
                turn_quad(1, 1)
            if t == 9:
                quantise_quad(1, 0)
                group_quad(1, 1, nc.scalar.copy)
            if t == 10:
                quantise_quad(1, 1)
